import numpy as np
import ml_dtypes


def mxq(x, axis, fmt="e4m3"):
    dtype, down = {"e4m3": (ml_dtypes.float8_e4m3fn, 7), "e5m2": (ml_dtypes.float8_e5m2, 14)}[fmt]
    v = np.moveaxis(np.asarray(x, np.float32).astype(ml_dtypes.bfloat16).astype(np.float64), axis, -1)
    blocks = v.reshape(v.shape[:-1] + (-1, 32))
    amax = np.abs(blocks).max(-1, keepdims=True)
    byte = np.maximum(np.where(amax > 0, np.frexp(amax)[1] - 1 + 127, 0) - down, 1)
    scale = np.exp2(byte - 127.0)
    codes = (blocks / scale).astype(np.float32).astype(dtype).astype(np.float64)
    return np.moveaxis((codes * scale).reshape(v.shape), -1, axis)


WIDE = False


def mx_kscale(k):
    if not WIDE:
        return np.ones(k)
    levels = np.array([10, -10, 5, -5, 0])
    a = np.random.permutation(np.resize(levels, k // 512 * 4)).reshape(k // 512, 4)
    idx = np.arange(k)
    return np.exp2(a[idx // 512, idx % 128 // 32])


BF16 = ml_dtypes.bfloat16


def bf(x):
    return np.asarray(x, np.float32).astype(BF16)


def f64(x):
    return np.asarray(x).astype(np.float64)


E2M1 = np.array([0.0, 0.5, 1.0, 1.5, 2.0, 3.0, 4.0, 6.0, -0.0, -0.5, -1.0, -1.5, -2.0, -3.0, -4.0, -6.0])


def pack_weight(w, fmt):
    k, n = w.shape
    w = f64(bf(w)).reshape(k // 32, 32, n)
    amax = np.abs(w).max(1)
    if fmt == "e4m3":
        byte = np.frexp(amax)[1] - 1 + 127 - 7
    else:
        mant, ex = np.frexp(amax / 6.0)
        byte = np.where(mant > 0.5, ex, ex - 1) + 127
    byte = np.clip(np.where(amax > 0, byte, 1), 1, 254)
    scaled = (w * np.exp2(127.0 - byte)[:, None, :]).reshape(k, n).astype(np.float32)
    by_word = np.ascontiguousarray(scaled.reshape(k // 512, 128, 4, n).transpose(0, 1, 3, 2))
    if fmt == "e4m3":
        words = by_word.astype(ml_dtypes.float8_e4m3fn).view(np.uint8)
    else:
        c = by_word.astype(ml_dtypes.float4_e2m1fn).view(np.uint8) & 0xF
        words = c[..., 0::2] | (c[..., 1::2] << 4)
    return np.ascontiguousarray(words), np.ascontiguousarray(byte.astype(np.uint8).reshape(k // 512, 16, n))


def unpack_weight(words, scales, fmt):
    g, p, n, _ = words.shape
    if fmt == "e4m3":
        vals = np.ascontiguousarray(words).view(ml_dtypes.float8_e4m3fn).astype(np.float64)
    else:
        nib = np.empty((g, p, n, 4), np.uint8)
        nib[..., 0::2] = words & 0xF
        nib[..., 1::2] = words >> 4
        vals = E2M1[nib]
    vals = vals * np.repeat(np.exp2(scales.astype(np.float64) - 127.0), 8, axis=1)[..., None]
    return vals.transpose(0, 1, 3, 2).reshape(g * 512, n)

def pack4(w):
    words, scales = pack_weight(w, "e2m1")
    return words.reshape(words.shape[0], 128, -1), scales


def unpack4(words, scales):
    return unpack_weight(words.reshape(words.shape[0], 128, -1, 2), scales, "e2m1")


B, IN, L = 256, 2048, 1536


def sigmoid(v):
    return 1.0 / (1.0 + np.exp(-v))


def setup_inputs():
    s = mx_kscale(IN)
    inp = bf(np.random.standard_normal((B, IN)) * s)
    h0 = bf(np.random.standard_normal((B, L)))
    gh0 = bf(np.random.standard_normal((B, 3 * L)) * 0.75)
    w = np.random.standard_normal((3 * L, IN)) * 0.7 / np.sqrt(IN) / s
    words, scales = pack4(w.T)
    b_ih0 = bf(np.random.standard_normal(3 * L) * 0.3)
    return {"input": inp,
            "h0": h0,
            "gh0": gh0,
            "W_ih0_words": words,
            "W_ih0_scales": scales,
            "b_ih0": b_ih0}


def reference(input, h0, gh0, W_ih0_words, W_ih0_scales, b_ih0):
    h, gh = f64(h0), f64(gh0)
    gi = (mxq(f64(input), 1, "e4m3") @ unpack4(W_ih0_words, W_ih0_scales)) + f64(b_ih0)
    i_r, i_z, i_n = gi[:, :L], gi[:, L:2 * L], gi[:, 2 * L:]
    h_r, h_z, h_n = gh[:, :L], gh[:, L:2 * L], gh[:, 2 * L:]
    r = sigmoid(i_r + h_r)
    z = sigmoid(i_z + h_z)
    n = np.tanh(i_n + r * h_n)
    return (1.0 - z) * n + z * h

@@ -1,0 +1,182 @@
+from contextlib import ExitStack
+
+import concourse.mybir as mybir
+from concourse.masks import make_identity
+
+F32 = mybir.dt.float32
+BF16 = mybir.dt.bfloat16
+I32 = mybir.dt.int32
+U32 = mybir.dt.uint32
+U8 = mybir.dt.uint8
+FP8X4 = mybir.dt.float8_e4m3fn_x4
+FP4X4 = mybir.dt.float4_e2m1fn_x4
+ACT = mybir.ActivationFunctionType
+ALU = mybir.AluOpType
+
+P = 128
+B, IN, L = 256, 2048, 1536
+K_PASS = 4 * P
+PASSES = IN // K_PASS
+ROW_TILES = B // P
+N_TILE = 512
+COL_TILES = L // N_TILE
+GATES = ("r", "n", "z")
+GATE_COLUMN = {"r": 0, "z": L, "n": 2 * L}
+QUADRANTS = 4
+
+FLOPS = 2 * B * IN * 3 * L
+
+
+def tile_grucellstack_pa_kernel(tc, x, h0, gh0, w_words, w_scales, b_ih0, out):
+    nc = tc.nc
+    chunks = [(gate, j) for j in range(COL_TILES) for gate in GATES]
+
+    with ExitStack() as stack:
+        keep = stack.enter_context(tc.tile_pool(name="keep", bufs=1))
+        work = stack.enter_context(tc.tile_pool(name="work", bufs=4))
+        psum = stack.enter_context(tc.psum_pool(name="psum", bufs=8))
+
+        x_rows = [keep.tile([P, IN], BF16, name="x_rows%d" % m) for m in range(ROW_TILES)]
+        x_grouped = [keep.tile([P, IN], BF16, name="x_grouped%d" % m, align_bytes=64) for m in range(ROW_TILES)]
+        x_codes = [keep.tile([P, IN // 4], U32, name="x_codes%d" % m, align_bytes=64) for m in range(ROW_TILES)]
+        x_scales = [keep.tile([P, IN // 4], U8, name="x_scales%d" % m, align_bytes=64) for m in range(ROW_TILES)]
+        w_codes = {}
+        w_planes = {}
+        gh_block = {}
+        for gate, j in chunks:
+            w_codes[(gate, j)] = keep.tile([P, PASSES, 2 * N_TILE], U8, name="w_codes_%s%d" % (gate, j), align_bytes=64)
+            w_planes[(gate, j)] = keep.tile([P, PASSES, N_TILE], U8, name="w_plane_%s%d" % (gate, j), align_bytes=64)
+            gh_block[(gate, j)] = keep.tile([P, ROW_TILES, N_TILE], BF16, name="gh_%s%d" % (gate, j))
+        h_block = [keep.tile([P, ROW_TILES, N_TILE], BF16, name="h_%d" % j) for j in range(COL_TILES)]
+        bias_row = keep.tile([P, 3 * L], BF16, name="bias_row")
+        ones = keep.tile([P, P], BF16, name="ones")
+        ident_bf16 = keep.tile([P, P], BF16, name="ident_bf16")
+        ident_f32 = keep.tile([P, P], F32, name="ident_f32")
+        table_in = keep.tile([P, 1], F32, name="table_in")
+        table_out = keep.tile([P, 1], F32, name="table_out")
+
+        nc.vector.memset(bias_row[:].bitcast(I32), 0)
+        for chunk in chunks:
+            nc.vector.memset(w_planes[chunk][:].bitcast(I32), 0)
+        nc.vector.memset(ones[:], 1.0)
+        nc.vector.memset(table_in[:], 0.0)
+        make_identity(nc, ident_f32[:])
+        make_identity(nc, ident_bf16[:])
+        nc.scalar.activation(out=table_out[:], in_=table_in[:], func=ACT.Sigmoid)
+
+        for m in range(ROW_TILES):
+            nc.sync.dma_start(out=x_rows[m][:], in_=x[m * P : (m + 1) * P, :])
+        nc.sync.dma_start(out=bias_row[0:1, :], in_=b_ih0.rearrange("(o c) -> o c", o=1))
+
+        scale_rows = w_scales.bitcast(I32).rearrange("g (Q s) c -> s Q g c", s=4)
+        word_rows = w_words.bitcast(I32).rearrange("g p c -> p g c")
+        gh_rows = gh0.rearrange("(m p) c -> p m c", p=P)
+        h_rows = h0.rearrange("(m p) c -> p m c", p=P)
+        for gate, j in chunks:
+            first = GATE_COLUMN[gate] + j * N_TILE
+            plane_words = w_planes[(gate, j)][:].bitcast(I32)
+            for s in range(4):
+                nc.sync.dma_start(
+                    out=plane_words[s : P : P // QUADRANTS, :, :],
+                    in_=scale_rows[s][:, :, first // 4 : (first + N_TILE) // 4],
+                )
+            nc.sync.dma_start(out=gh_block[(gate, j)][:], in_=gh_rows[:, :, first : first + N_TILE])
+            if gate == "n":
+                nc.sync.dma_start(out=h_block[j][:], in_=h_rows[:, :, j * N_TILE : (j + 1) * N_TILE])
+            nc.sync.dma_start(
+                out=w_codes[(gate, j)][:].bitcast(I32),
+                in_=word_rows[:, :, first // 2 : (first + N_TILE) // 2],
+            )
+
+        halves = 2
+        for m in range(ROW_TILES):
+            x_pairs = x_rows[m][:].bitcast(F32)
+            grouped_pairs = x_grouped[m][:].bitcast(F32)
+            for half in range(halves):
+                flipped = psum.tile([P, N_TILE], F32, tag="bank", name="flipped")
+                for slot in range(4):
+                    g = half * 2 + slot // 2
+                    u = slot % 2
+                    nc.tensor.transpose(
+                        out=flipped[:, slot * P : (slot + 1) * P],
+                        in_=x_pairs[:, 256 * g + u : 256 * (g + 1) : 2],
+                        identity=ident_f32[:],
+                    )
+                source = flipped[:].rearrange("p (g u b) -> p g b u", g=2, u=2)
+                target = grouped_pairs[:, half * N_TILE : (half + 1) * N_TILE].rearrange(
+                    "p (g b u) -> p g b u", g=2, u=2
+                )
+                if half == 0:
+                    nc.vector.tensor_copy(out=target, in_=source)
+                else:
+                    nc.scalar.copy(out=target, in_=source)
+            for half in range(halves):
+                values = slice(half * IN // 2, (half + 1) * IN // 2)
+                words = slice(half * IN // 8, (half + 1) * IN // 8)
+                nc.vector.quantize_mx(
+                    out=x_codes[m][:, words].bitcast(FP8X4),
+                    scales=x_scales[m][:, words],
+                    in_=x_grouped[m][:, values],
+                )
+
+        def gi_bank(gate, j, m):
+            acc = psum.tile([P, N_TILE], F32, tag="bank", name="acc")
+            for g in range(PASSES):
+                rows = slice(g * P, (g + 1) * P)
+                nc.tensor.matmul_mx(
+                    out=acc[:],
+                    lhsT=x_codes[m][:, rows].bitcast(FP8X4),
+                    lhsT_scale=x_scales[m][:, rows],
+                    rhs=w_codes[(gate, j)][:, g, :].bitcast(FP4X4),
+                    rhs_scale=w_planes[(gate, j)][:, g, :],
+                    start=(g == 0),
+                    stop=(g == PASSES - 1),
+                )
+            return acc
+
+        def bias_columns(gate, j):
+            first = GATE_COLUMN[gate] + j * N_TILE
+            return bias_row[:, first : first + N_TILE]
+
+        def gh_plus_bias(gate, j, m, tag):
+            bank = psum.tile([P, N_TILE], F32, tag="bank", name="gh_bias")
+            nc.tensor.matmul(out=bank[:], lhsT=ident_bf16[:], rhs=gh_block[(gate, j)][:, m, :], start=True, stop=False)
+            nc.tensor.matmul(out=bank[:], lhsT=ones[:], rhs=bias_columns(gate, j), start=False, stop=True)
+            total = work.tile([P, N_TILE], F32, tag=tag, name="gate_" + tag)
+            nc.scalar.copy(out=total[:], in_=bank[:])
+            return total
+
+        def sigmoid_gate(gate, j, m):
+            value = gh_plus_bias(gate, j, m, gate)
+            acc = gi_bank(gate, j, m)
+            nc.vector.tensor_tensor(out=value[:], in0=acc[:], in1=value[:], op=ALU.add)
+            nc.scalar.activation(out=value[:], in_=value[:], func=ACT.Sigmoid)
+            return value
+
+        for j in range(COL_TILES):
+            r = [sigmoid_gate("r", j, m) for m in range(ROW_TILES)]
+
+            bias_n = psum.tile([P, N_TILE], F32, tag="bank", name="bias_n")
+            nc.tensor.matmul(out=bias_n[:], lhsT=ones[:], rhs=bias_columns("n", j), start=True, stop=True)
+            n = []
+            side = []
+            for m in range(ROW_TILES):
+                s_m = work.tile([P, N_TILE], F32, tag="side", name="side")
+                nc.vector.tensor_tensor(out=s_m[:], in0=r[m][:], in1=gh_block[("n", j)][:, m, :], op=ALU.mult)
+                nc.vector.tensor_tensor(out=s_m[:], in0=bias_n[:], in1=s_m[:], op=ALU.add)
+                side.append(s_m)
+            for m in range(ROW_TILES):
+                acc = gi_bank("n", j, m)
+                n_m = work.tile([P, N_TILE], F32, tag="n", name="n")
+                nc.vector.tensor_tensor(out=n_m[:], in0=acc[:], in1=side[m][:], op=ALU.add)
+                nc.scalar.activation(out=n_m[:], in_=n_m[:], func=ACT.Tanh)
+                n.append(n_m)
+            for m in range(ROW_TILES):
+                nc.vector.tensor_tensor(out=side[m][:], in0=h_block[j][:, m, :], in1=n[m][:], op=ALU.subtract)
+
+            z = [sigmoid_gate("z", j, m) for m in range(ROW_TILES)]
+            for m in range(ROW_TILES):
+                nc.vector.tensor_tensor(out=side[m][:], in0=z[m][:], in1=side[m][:], op=ALU.mult)
+            for m in range(ROW_TILES):
+                nc.vector.tensor_tensor(out=n[m][:], in0=n[m][:], in1=side[m][:], op=ALU.add)
+                nc.sync.dma_start(out=out[m * P : (m + 1) * P, j * N_TILE : (j + 1) * N_TILE], in_=n[m][:])

@@ -162,7 +162,7 @@ def tile_grucellstack_pa_kernel(tc, x, h0, gh0, w_words, w_scales, b_ih0, out):
             side = []
             for m in range(ROW_TILES):
                 s_m = work.tile([P, N_TILE], F32, tag="side", name="side")
-                nc.vector.tensor_tensor(out=s_m[:], in0=r[m][:], in1=gh_block[("n", j)][:, m, :], op=ALU.mult)
+                nc.gpsimd.tensor_tensor(out=s_m[:], in0=r[m][:], in1=gh_block[("n", j)][:, m, :], op=ALU.mult)
                 nc.vector.tensor_tensor(out=s_m[:], in0=bias_n[:], in1=s_m[:], op=ALU.add)
                 side.append(s_m)
             for m in range(ROW_TILES):
@@ -172,7 +172,7 @@ def tile_grucellstack_pa_kernel(tc, x, h0, gh0, w_words, w_scales, b_ih0, out):
                 nc.scalar.activation(out=n_m[:], in_=n_m[:], func=ACT.Tanh)
                 n.append(n_m)
             for m in range(ROW_TILES):
-                nc.vector.tensor_tensor(out=side[m][:], in0=h_block[j][:, m, :], in1=n[m][:], op=ALU.subtract)
+                nc.gpsimd.tensor_tensor(out=side[m][:], in0=h_block[j][:, m, :], in1=n[m][:], op=ALU.subtract)
 
             z = [sigmoid_gate("z", j, m) for m in range(ROW_TILES)]
             for m in range(ROW_TILES):

@@ -23,23 +23,26 @@ COL_TILES = L // N_TILE
 GATES = ("r", "n", "z")
 GATE_COLUMN = {"r": 0, "z": L, "n": 2 * L}
 QUADRANTS = 4
+PSUM_BANKS = 8
 
 FLOPS = 2 * B * IN * 3 * L
 
 
 def tile_grucellstack_pa_kernel(tc, x, h0, gh0, w_words, w_scales, b_ih0, out):
     nc = tc.nc
+    row_tiles = range(ROW_TILES)
     chunks = [(gate, j) for j in range(COL_TILES) for gate in GATES]
 
     with ExitStack() as stack:
         keep = stack.enter_context(tc.tile_pool(name="keep", bufs=1))
-        work = stack.enter_context(tc.tile_pool(name="work", bufs=4))
-        psum = stack.enter_context(tc.psum_pool(name="psum", bufs=8))
+        work = stack.enter_context(tc.tile_pool(name="work", bufs=2 * ROW_TILES))
+        psum = stack.enter_context(tc.psum_pool(name="psum", bufs=PSUM_BANKS))
+        stack.enter_context(tc.manual_schedule())
 
-        x_rows = [keep.tile([P, IN], BF16, name="x_rows%d" % m) for m in range(ROW_TILES)]
-        x_grouped = [keep.tile([P, IN], BF16, name="x_grouped%d" % m, align_bytes=64) for m in range(ROW_TILES)]
-        x_codes = [keep.tile([P, IN // 4], U32, name="x_codes%d" % m, align_bytes=64) for m in range(ROW_TILES)]
-        x_scales = [keep.tile([P, IN // 4], U8, name="x_scales%d" % m, align_bytes=64) for m in range(ROW_TILES)]
+        x_rows = [keep.tile([P, IN], BF16, name="x_rows%d" % m) for m in row_tiles]
+        x_grouped = [keep.tile([P, IN], BF16, name="x_grouped%d" % m, align_bytes=64) for m in row_tiles]
+        x_codes = [keep.tile([P, IN // 4], U32, name="x_codes%d" % m, align_bytes=64) for m in row_tiles]
+        x_scales = [keep.tile([P, IN // 4], U8, name="x_scales%d" % m, align_bytes=64) for m in row_tiles]
         w_codes = {}
         w_planes = {}
         gh_block = {}
@@ -55,24 +58,21 @@ def tile_grucellstack_pa_kernel(tc, x, h0, gh0, w_words, w_scales, b_ih0, out):
         table_in = keep.tile([P, 1], F32, name="table_in")
         table_out = keep.tile([P, 1], F32, name="table_out")
 
+        nc.vector.memset(table_in[:], 0.0)
+        nc.scalar.activation(out=table_out[:], in_=table_in[:], func=ACT.Sigmoid)
         nc.vector.memset(bias_row[:].bitcast(I32), 0)
+        nc.vector.memset(ones[:], 1.0)
         for chunk in chunks:
             nc.vector.memset(w_planes[chunk][:].bitcast(I32), 0)
-        nc.vector.memset(ones[:], 1.0)
-        nc.vector.memset(table_in[:], 0.0)
         make_identity(nc, ident_f32[:])
         make_identity(nc, ident_bf16[:])
-        nc.scalar.activation(out=table_out[:], in_=table_in[:], func=ACT.Sigmoid)
-
-        for m in range(ROW_TILES):
-            nc.sync.dma_start(out=x_rows[m][:], in_=x[m * P : (m + 1) * P, :])
-        nc.sync.dma_start(out=bias_row[0:1, :], in_=b_ih0.rearrange("(o c) -> o c", o=1))
 
         scale_rows = w_scales.bitcast(I32).rearrange("g (Q s) c -> s Q g c", s=4)
         word_rows = w_words.bitcast(I32).rearrange("g p c -> p g c")
         gh_rows = gh0.rearrange("(m p) c -> p m c", p=P)
         h_rows = h0.rearrange("(m p) c -> p m c", p=P)
-        for gate, j in chunks:
+
+        def load_scales(gate, j):
             first = GATE_COLUMN[gate] + j * N_TILE
             plane_words = w_planes[(gate, j)][:].bitcast(I32)
             for s in range(4):
@@ -80,16 +80,35 @@ def tile_grucellstack_pa_kernel(tc, x, h0, gh0, w_words, w_scales, b_ih0, out):
                     out=plane_words[s : P : P // QUADRANTS, :, :],
                     in_=scale_rows[s][:, :, first // 4 : (first + N_TILE) // 4],
                 )
-            nc.sync.dma_start(out=gh_block[(gate, j)][:], in_=gh_rows[:, :, first : first + N_TILE])
-            if gate == "n":
-                nc.sync.dma_start(out=h_block[j][:], in_=h_rows[:, :, j * N_TILE : (j + 1) * N_TILE])
+
+        def load_words(gate, j):
+            first = GATE_COLUMN[gate] + j * N_TILE
             nc.sync.dma_start(
                 out=w_codes[(gate, j)][:].bitcast(I32),
                 in_=word_rows[:, :, first // 2 : (first + N_TILE) // 2],
             )
 
+        def load_gh(gate, j):
+            first = GATE_COLUMN[gate] + j * N_TILE
+            nc.sync.dma_start(out=gh_block[(gate, j)][:], in_=gh_rows[:, :, first : first + N_TILE])
+
+        for m in row_tiles:
+            nc.sync.dma_start(out=x_rows[m][:], in_=x[m * P : (m + 1) * P, :])
+        nc.sync.dma_start(out=bias_row[0:1, :], in_=b_ih0.rearrange("(o c) -> o c", o=1))
+        for j in range(COL_TILES):
+            load_scales("r", j)
+            load_gh("r", j)
+            load_words("r", j)
+            load_scales("n", j)
+            load_gh("n", j)
+            load_gh("z", j)
+            load_words("n", j)
+            load_scales("z", j)
+            nc.sync.dma_start(out=h_block[j][:], in_=h_rows[:, :, j * N_TILE : (j + 1) * N_TILE])
+            load_words("z", j)
+
         halves = 2
-        for m in range(ROW_TILES):
+        for m in row_tiles:
             x_pairs = x_rows[m][:].bitcast(F32)
             grouped_pairs = x_grouped[m][:].bitcast(F32)
             for half in range(halves):
@@ -110,6 +129,7 @@ def tile_grucellstack_pa_kernel(tc, x, h0, gh0, w_words, w_scales, b_ih0, out):
                     nc.vector.tensor_copy(out=target, in_=source)
                 else:
                     nc.scalar.copy(out=target, in_=source)
+        for m in row_tiles:
             for half in range(halves):
                 values = slice(half * IN // 2, (half + 1) * IN // 2)
                 words = slice(half * IN // 8, (half + 1) * IN // 8)
@@ -119,64 +139,69 @@ def tile_grucellstack_pa_kernel(tc, x, h0, gh0, w_words, w_scales, b_ih0, out):
                     in_=x_grouped[m][:, values],
                 )
 
-        def gi_bank(gate, j, m):
-            acc = psum.tile([P, N_TILE], F32, tag="bank", name="acc")
-            for g in range(PASSES):
-                rows = slice(g * P, (g + 1) * P)
-                nc.tensor.matmul_mx(
-                    out=acc[:],
-                    lhsT=x_codes[m][:, rows].bitcast(FP8X4),
-                    lhsT_scale=x_scales[m][:, rows],
-                    rhs=w_codes[(gate, j)][:, g, :].bitcast(FP4X4),
-                    rhs_scale=w_planes[(gate, j)][:, g, :],
-                    start=(g == 0),
-                    stop=(g == PASSES - 1),
-                )
-            return acc
-
         def bias_columns(gate, j):
             first = GATE_COLUMN[gate] + j * N_TILE
             return bias_row[:, first : first + N_TILE]
 
-        def gh_plus_bias(gate, j, m, tag):
-            bank = psum.tile([P, N_TILE], F32, tag="bank", name="gh_bias")
-            nc.tensor.matmul(out=bank[:], lhsT=ident_bf16[:], rhs=gh_block[(gate, j)][:, m, :], start=True, stop=False)
-            nc.tensor.matmul(out=bank[:], lhsT=ones[:], rhs=bias_columns(gate, j), start=False, stop=True)
-            total = work.tile([P, N_TILE], F32, tag=tag, name="gate_" + tag)
-            nc.scalar.copy(out=total[:], in_=bank[:])
-            return total
+        def gi_banks(gate, j):
+            banks = []
+            for m in row_tiles:
+                acc = psum.tile([P, N_TILE], F32, tag="bank", name="acc")
+                for g in range(PASSES):
+                    rows = slice(g * P, (g + 1) * P)
+                    nc.tensor.matmul_mx(
+                        out=acc[:],
+                        lhsT=x_codes[m][:, rows].bitcast(FP8X4),
+                        lhsT_scale=x_scales[m][:, rows],
+                        rhs=w_codes[(gate, j)][:, g, :].bitcast(FP4X4),
+                        rhs_scale=w_planes[(gate, j)][:, g, :],
+                        start=(g == 0),
+                        stop=(g == PASSES - 1),
+                    )
+                banks.append(acc)
+            return banks
 
-        def sigmoid_gate(gate, j, m):
-            value = gh_plus_bias(gate, j, m, gate)
-            acc = gi_bank(gate, j, m)
-            nc.vector.tensor_tensor(out=value[:], in0=acc[:], in1=value[:], op=ALU.add)
-            nc.scalar.activation(out=value[:], in_=value[:], func=ACT.Sigmoid)
-            return value
+        def gh_plus_bias(gate, j):
+            totals = []
+            for m in row_tiles:
+                bank = psum.tile([P, N_TILE], F32, tag="bank", name="gh_bias")
+                nc.tensor.matmul(out=bank[:], lhsT=ident_bf16[:], rhs=gh_block[(gate, j)][:, m, :], start=True, stop=False)
+                nc.tensor.matmul(out=bank[:], lhsT=ones[:], rhs=bias_columns(gate, j), start=False, stop=True)
+                total = work.tile([P, N_TILE], F32, tag=gate, name="gate_" + gate)
+                nc.scalar.copy(out=total[:], in_=bank[:])
+                totals.append(total)
+            return totals
+
+        def sigmoid_of_sum(banks, totals):
+            for m in row_tiles:
+                nc.vector.tensor_tensor(out=totals[m][:], in0=banks[m][:], in1=totals[m][:], op=ALU.add)
+                nc.scalar.activation(out=totals[m][:], in_=totals[m][:], func=ACT.Sigmoid)
 
         for j in range(COL_TILES):
-            r = [sigmoid_gate("r", j, m) for m in range(ROW_TILES)]
+            r = gh_plus_bias("r", j)
+            sigmoid_of_sum(gi_banks("r", j), r)
 
             bias_n = psum.tile([P, N_TILE], F32, tag="bank", name="bias_n")
             nc.tensor.matmul(out=bias_n[:], lhsT=ones[:], rhs=bias_columns("n", j), start=True, stop=True)
-            n = []
-            side = []
-            for m in range(ROW_TILES):
-                s_m = work.tile([P, N_TILE], F32, tag="side", name="side")
-                nc.gpsimd.tensor_tensor(out=s_m[:], in0=r[m][:], in1=gh_block[("n", j)][:, m, :], op=ALU.mult)
-                nc.vector.tensor_tensor(out=s_m[:], in0=bias_n[:], in1=s_m[:], op=ALU.add)
-                side.append(s_m)
-            for m in range(ROW_TILES):
-                acc = gi_bank("n", j, m)
-                n_m = work.tile([P, N_TILE], F32, tag="n", name="n")
-                nc.vector.tensor_tensor(out=n_m[:], in0=acc[:], in1=side[m][:], op=ALU.add)
-                nc.scalar.activation(out=n_m[:], in_=n_m[:], func=ACT.Tanh)
-                n.append(n_m)
-            for m in range(ROW_TILES):
-                nc.gpsimd.tensor_tensor(out=side[m][:], in0=h_block[j][:, m, :], in1=n[m][:], op=ALU.subtract)
+            z = gh_plus_bias("z", j)
+            gi_n = gi_banks("n", j)
 
-            z = [sigmoid_gate("z", j, m) for m in range(ROW_TILES)]
-            for m in range(ROW_TILES):
+            side = [work.tile([P, N_TILE], F32, tag="side", name="side") for m in row_tiles]
+            n = [work.tile([P, N_TILE], F32, tag="n", name="n") for m in row_tiles]
+            for m in row_tiles:
+                nc.vector.tensor_tensor(out=side[m][:], in0=r[m][:], in1=gh_block[("n", j)][:, m, :], op=ALU.mult)
+            for m in row_tiles:
+                nc.vector.tensor_tensor(out=side[m][:], in0=bias_n[:], in1=side[m][:], op=ALU.add)
+            for m in row_tiles:
+                nc.vector.tensor_tensor(out=n[m][:], in0=gi_n[m][:], in1=side[m][:], op=ALU.add)
+                nc.scalar.activation(out=n[m][:], in_=n[m][:], func=ACT.Tanh)
+
+            sigmoid_of_sum(gi_banks("z", j), z)
+
+            for m in row_tiles:
+                nc.vector.tensor_tensor(out=side[m][:], in0=h_block[j][:, m, :], in1=n[m][:], op=ALU.subtract)
+            for m in row_tiles:
                 nc.vector.tensor_tensor(out=side[m][:], in0=z[m][:], in1=side[m][:], op=ALU.mult)
-            for m in range(ROW_TILES):
+            for m in row_tiles:
                 nc.vector.tensor_tensor(out=n[m][:], in0=n[m][:], in1=side[m][:], op=ALU.add)
                 nc.sync.dma_start(out=out[m * P : (m + 1) * P, j * N_TILE : (j + 1) * N_TILE], in_=n[m][:])

@@ -20,7 +20,7 @@ PASSES = IN // K_PASS
 ROW_TILES = B // P
 N_TILE = 512
 COL_TILES = L // N_TILE
-GATES = ("r", "n", "z")
+GATES = ("r", "z", "n")
 GATE_COLUMN = {"r": 0, "z": L, "n": 2 * L}
 QUADRANTS = 4
 PSUM_BANKS = 8
@@ -39,7 +39,7 @@ def tile_grucellstack_pa_kernel(tc, x, h0, gh0, w_words, w_scales, b_ih0, out):
         psum = stack.enter_context(tc.psum_pool(name="psum", bufs=PSUM_BANKS))
         stack.enter_context(tc.manual_schedule())
 
-        x_rows = [keep.tile([P, IN], BF16, name="x_rows%d" % m) for m in row_tiles]
+        x_rows = [[keep.tile([P, IN // 2], BF16, name="x_rows%d_%d" % (m, half)) for half in range(2)] for m in row_tiles]
         x_grouped = [keep.tile([P, IN], BF16, name="x_grouped%d" % m, align_bytes=64) for m in row_tiles]
         x_codes = [keep.tile([P, IN // 4], U32, name="x_codes%d" % m, align_bytes=64) for m in row_tiles]
         x_scales = [keep.tile([P, IN // 4], U8, name="x_scales%d" % m, align_bytes=64) for m in row_tiles]
@@ -60,12 +60,15 @@ def tile_grucellstack_pa_kernel(tc, x, h0, gh0, w_words, w_scales, b_ih0, out):
 
         nc.vector.memset(table_in[:], 0.0)
         nc.scalar.activation(out=table_out[:], in_=table_in[:], func=ACT.Sigmoid)
-        nc.vector.memset(bias_row[:].bitcast(I32), 0)
+        nc.vector.memset(w_planes[chunks[0]][:].bitcast(I32), 0)
         nc.vector.memset(ones[:], 1.0)
-        for chunk in chunks:
+        nc.vector.memset(bias_row[:].bitcast(I32), 0)
+        for chunk in chunks[1 : len(GATES)]:
             nc.vector.memset(w_planes[chunk][:].bitcast(I32), 0)
         make_identity(nc, ident_f32[:])
         make_identity(nc, ident_bf16[:])
+        for chunk in chunks[len(GATES) :]:
+            nc.gpsimd.memset(w_planes[chunk][:].bitcast(F32), 0.0)
 
         scale_rows = w_scales.bitcast(I32).rearrange("g (Q s) c -> s Q g c", s=4)
         word_rows = w_words.bitcast(I32).rearrange("g p c -> p g c")
@@ -93,28 +96,29 @@ def tile_grucellstack_pa_kernel(tc, x, h0, gh0, w_words, w_scales, b_ih0, out):
             nc.sync.dma_start(out=gh_block[(gate, j)][:], in_=gh_rows[:, :, first : first + N_TILE])
 
         for m in row_tiles:
-            nc.sync.dma_start(out=x_rows[m][:], in_=x[m * P : (m + 1) * P, :])
+            for half in range(2):
+                nc.sync.dma_start(out=x_rows[m][half][:], in_=x[m * P : (m + 1) * P, half * IN // 2 : (half + 1) * IN // 2])
         nc.sync.dma_start(out=bias_row[0:1, :], in_=b_ih0.rearrange("(o c) -> o c", o=1))
         for j in range(COL_TILES):
             load_scales("r", j)
             load_gh("r", j)
             load_words("r", j)
-            load_scales("n", j)
-            load_gh("n", j)
-            load_gh("z", j)
-            load_words("n", j)
             load_scales("z", j)
-            nc.sync.dma_start(out=h_block[j][:], in_=h_rows[:, :, j * N_TILE : (j + 1) * N_TILE])
+            load_gh("z", j)
+            load_gh("n", j)
             load_words("z", j)
+            nc.sync.dma_start(out=h_block[j][:], in_=h_rows[:, :, j * N_TILE : (j + 1) * N_TILE])
+            load_scales("n", j)
+            load_words("n", j)
 
         halves = 2
         for m in row_tiles:
-            x_pairs = x_rows[m][:].bitcast(F32)
             grouped_pairs = x_grouped[m][:].bitcast(F32)
             for half in range(halves):
+                x_pairs = x_rows[m][half][:].bitcast(F32)
                 flipped = psum.tile([P, N_TILE], F32, tag="bank", name="flipped")
                 for slot in range(4):
-                    g = half * 2 + slot // 2
+                    g = slot // 2
                     u = slot % 2
                     nc.tensor.transpose(
                         out=flipped[:, slot * P : (slot + 1) * P],
@@ -181,27 +185,36 @@ def tile_grucellstack_pa_kernel(tc, x, h0, gh0, w_words, w_scales, b_ih0, out):
             r = gh_plus_bias("r", j)
             sigmoid_of_sum(gi_banks("r", j), r)
 
-            bias_n = psum.tile([P, N_TILE], F32, tag="bank", name="bias_n")
-            nc.tensor.matmul(out=bias_n[:], lhsT=ones[:], rhs=bias_columns("n", j), start=True, stop=True)
-            z = gh_plus_bias("z", j)
-            gi_n = gi_banks("n", j)
+            z_sum = gh_plus_bias("z", j)
+            gi_z = gi_banks("z", j)
 
             side = [work.tile([P, N_TILE], F32, tag="side", name="side") for m in row_tiles]
-            n = [work.tile([P, N_TILE], F32, tag="n", name="n") for m in row_tiles]
             for m in row_tiles:
                 nc.vector.tensor_tensor(out=side[m][:], in0=r[m][:], in1=gh_block[("n", j)][:, m, :], op=ALU.mult)
+
+            z = [work.tile([P, N_TILE], F32, tag="zgate", name="zgate") for m in row_tiles]
+            z_rest = [work.tile([P, N_TILE], F32, tag="zrest", name="zrest") for m in row_tiles]
+            z_h = [work.tile([P, N_TILE], F32, tag="zh", name="zh") for m in row_tiles]
+            for m in row_tiles:
+                nc.vector.tensor_tensor(out=z_sum[m][:], in0=gi_z[m][:], in1=z_sum[m][:], op=ALU.add)
+                nc.scalar.activation(out=z[m][:], in_=z_sum[m][:], func=ACT.Sigmoid)
+                nc.gpsimd.tensor_tensor(out=z_h[m][:], in0=z[m][:], in1=h_block[j][:, m, :], op=ALU.mult)
+            for m in row_tiles:
+                nc.scalar.activation(out=z_rest[m][:], in_=z_sum[m][:], func=ACT.Sigmoid, scale=-1.0)
+
+            bias_n = psum.tile([P, N_TILE], F32, tag="bank", name="bias_n")
+            nc.tensor.matmul(out=bias_n[:], lhsT=ones[:], rhs=bias_columns("n", j), start=True, stop=True)
+            gi_n = gi_banks("n", j)
+
+            n = [work.tile([P, N_TILE], F32, tag="n", name="n") for m in row_tiles]
             for m in row_tiles:
                 nc.vector.tensor_tensor(out=side[m][:], in0=bias_n[:], in1=side[m][:], op=ALU.add)
             for m in row_tiles:
                 nc.vector.tensor_tensor(out=n[m][:], in0=gi_n[m][:], in1=side[m][:], op=ALU.add)
                 nc.scalar.activation(out=n[m][:], in_=n[m][:], func=ACT.Tanh)
 
-            sigmoid_of_sum(gi_banks("z", j), z)
-
             for m in row_tiles:
-                nc.vector.tensor_tensor(out=side[m][:], in0=h_block[j][:, m, :], in1=n[m][:], op=ALU.subtract)
+                nc.vector.tensor_tensor(out=n[m][:], in0=z_rest[m][:], in1=n[m][:], op=ALU.mult)
             for m in row_tiles:
-                nc.vector.tensor_tensor(out=side[m][:], in0=z[m][:], in1=side[m][:], op=ALU.mult)
-            for m in row_tiles:
-                nc.vector.tensor_tensor(out=n[m][:], in0=n[m][:], in1=side[m][:], op=ALU.add)
+                nc.vector.tensor_tensor(out=n[m][:], in0=n[m][:], in1=z_h[m][:], op=ALU.add)
                 nc.sync.dma_start(out=out[m * P : (m + 1) * P, j * N_TILE : (j + 1) * N_TILE], in_=n[m][:])

@@ -183,14 +183,19 @@ def tile_grucellstack_pa_kernel(tc, x, h0, gh0, w_words, w_scales, b_ih0, out):
 
         for j in range(COL_TILES):
             r = gh_plus_bias("r", j)
-            sigmoid_of_sum(gi_banks("r", j), r)
-
-            z_sum = gh_plus_bias("z", j)
-            gi_z = gi_banks("z", j)
-
+            gi_r = gi_banks("r", j)
             side = [work.tile([P, N_TILE], F32, tag="side", name="side") for m in row_tiles]
             for m in row_tiles:
-                nc.vector.tensor_tensor(out=side[m][:], in0=r[m][:], in1=gh_block[("n", j)][:, m, :], op=ALU.mult)
+                nc.vector.tensor_tensor(out=r[m][:], in0=gi_r[m][:], in1=r[m][:], op=ALU.add)
+                nc.scalar.activation(out=r[m][:], in_=r[m][:], func=ACT.Sigmoid)
+                nc.gpsimd.tensor_tensor(out=side[m][:], in0=r[m][:], in1=gh_block[("n", j)][:, m, :], op=ALU.mult)
+
+            bias_z = psum.tile([P, N_TILE], F32, tag="bank", name="bias_z")
+            nc.tensor.matmul(out=bias_z[:], lhsT=ones[:], rhs=bias_columns("z", j), start=True, stop=True)
+            z_sum = [work.tile([P, N_TILE], F32, tag="z", name="z_sum") for m in row_tiles]
+            for m in row_tiles:
+                nc.vector.tensor_tensor(out=z_sum[m][:], in0=bias_z[:], in1=gh_block[("z", j)][:, m, :], op=ALU.add)
+            gi_z = gi_banks("z", j)
 
             z = [work.tile([P, N_TILE], F32, tag="zgate", name="zgate") for m in row_tiles]
             z_rest = [work.tile([P, N_TILE], F32, tag="zrest", name="zrest") for m in row_tiles]

@@ -50,6 +50,7 @@ def tile_grucellstack_pa_kernel(tc, x, h0, gh0, w_words, w_scales, b_ih0, out):
             w_codes[(gate, j)] = keep.tile([P, PASSES, 2 * N_TILE], U8, name="w_codes_%s%d" % (gate, j), align_bytes=64)
             w_planes[(gate, j)] = keep.tile([P, PASSES, N_TILE], U8, name="w_plane_%s%d" % (gate, j), align_bytes=64)
             gh_block[(gate, j)] = keep.tile([P, ROW_TILES, N_TILE], BF16, name="gh_%s%d" % (gate, j))
+        last_codes = [keep.tile([P, 2 * N_TILE], U8, name="last_codes%d" % g, align_bytes=64) for g in range(PASSES)]
         h_block = [keep.tile([P, ROW_TILES, N_TILE], BF16, name="h_%d" % j) for j in range(COL_TILES)]
         bias_row = keep.tile([P, 3 * L], BF16, name="bias_row")
         ones = keep.tile([P, P], BF16, name="ones")
@@ -107,9 +108,19 @@ def tile_grucellstack_pa_kernel(tc, x, h0, gh0, w_words, w_scales, b_ih0, out):
             load_gh("z", j)
             load_gh("n", j)
             load_words("z", j)
-            nc.sync.dma_start(out=h_block[j][:], in_=h_rows[:, :, j * N_TILE : (j + 1) * N_TILE])
-            load_scales("n", j)
-            load_words("n", j)
+            if j < COL_TILES - 1:
+                nc.sync.dma_start(out=h_block[j][:], in_=h_rows[:, :, j * N_TILE : (j + 1) * N_TILE])
+                load_scales("n", j)
+                load_words("n", j)
+            else:
+                load_scales("n", j)
+                first = GATE_COLUMN["n"] + j * N_TILE
+                for g in range(PASSES):
+                    nc.sync.dma_start(
+                        out=last_codes[g][:].bitcast(I32),
+                        in_=word_rows[:, g, first // 2 : (first + N_TILE) // 2],
+                    )
+                nc.sync.dma_start(out=h_block[j][:], in_=h_rows[:, :, j * N_TILE : (j + 1) * N_TILE])
 
         halves = 2
         for m in row_tiles:
@@ -165,6 +176,23 @@ def tile_grucellstack_pa_kernel(tc, x, h0, gh0, w_words, w_scales, b_ih0, out):
                 banks.append(acc)
             return banks
 
+        def last_banks():
+            gate, j = "n", COL_TILES - 1
+            banks = [psum.tile([P, N_TILE], F32, tag="bank", name="acc") for m in row_tiles]
+            for g in range(PASSES):
+                rows = slice(g * P, (g + 1) * P)
+                for m in row_tiles:
+                    nc.tensor.matmul_mx(
+                        out=banks[m][:],
+                        lhsT=x_codes[m][:, rows].bitcast(FP8X4),
+                        lhsT_scale=x_scales[m][:, rows],
+                        rhs=last_codes[g][:].bitcast(FP4X4),
+                        rhs_scale=w_planes[(gate, j)][:, g, :],
+                        start=(g == 0),
+                        stop=(g == PASSES - 1),
+                    )
+            return banks
+
         def gh_plus_bias(gate, j):
             totals = []
             for m in row_tiles:
@@ -209,7 +237,7 @@ def tile_grucellstack_pa_kernel(tc, x, h0, gh0, w_words, w_scales, b_ih0, out):
 
             bias_n = psum.tile([P, N_TILE], F32, tag="bank", name="bias_n")
             nc.tensor.matmul(out=bias_n[:], lhsT=ones[:], rhs=bias_columns("n", j), start=True, stop=True)
-            gi_n = gi_banks("n", j)
+            gi_n = gi_banks("n", j) if j < COL_TILES - 1 else last_banks()
 
             n = [work.tile([P, N_TILE], F32, tag="n", name="n") for m in row_tiles]
             for m in row_tiles:

@@ -100,27 +100,58 @@ def tile_grucellstack_pa_kernel(tc, x, h0, gh0, w_words, w_scales, b_ih0, out):
             for half in range(2):
                 nc.sync.dma_start(out=x_rows[m][half][:], in_=x[m * P : (m + 1) * P, half * IN // 2 : (half + 1) * IN // 2])
         nc.sync.dma_start(out=bias_row[0:1, :], in_=b_ih0.rearrange("(o c) -> o c", o=1))
-        for j in range(COL_TILES):
-            load_scales("r", j)
+        def load_h(j):
+            nc.sync.dma_start(out=h_block[j][:], in_=h_rows[:, :, j * N_TILE : (j + 1) * N_TILE])
+
+        def load_last_words():
+            first = GATE_COLUMN["n"] + (COL_TILES - 1) * N_TILE
+            for g in range(PASSES):
+                nc.sync.dma_start(out=last_codes[g][:].bitcast(I32), in_=word_rows[:, g, first // 2 : (first + N_TILE) // 2])
+
+        def load_scale(gate, j, s):
+            first = GATE_COLUMN[gate] + j * N_TILE
+            nc.sync.dma_start(
+                out=w_planes[(gate, j)][:].bitcast(I32)[s : P : P // QUADRANTS, :, :],
+                in_=scale_rows[s][:, :, first // 4 : (first + N_TILE) // 4],
+            )
+
+        for j in range(COL_TILES - 1):
+            load_scale("r", j, 0)
+            load_scale("r", j, 1)
             load_gh("r", j)
+            load_scale("r", j, 2)
+            load_scale("r", j, 3)
             load_words("r", j)
-            load_scales("z", j)
+            load_scale("z", j, 0)
+            load_scale("z", j, 1)
             load_gh("z", j)
+            load_scale("z", j, 2)
+            load_scale("z", j, 3)
             load_gh("n", j)
             load_words("z", j)
-            if j < COL_TILES - 1:
-                nc.sync.dma_start(out=h_block[j][:], in_=h_rows[:, :, j * N_TILE : (j + 1) * N_TILE])
-                load_scales("n", j)
-                load_words("n", j)
-            else:
-                load_scales("n", j)
-                first = GATE_COLUMN["n"] + j * N_TILE
-                for g in range(PASSES):
-                    nc.sync.dma_start(
-                        out=last_codes[g][:].bitcast(I32),
-                        in_=word_rows[:, g, first // 2 : (first + N_TILE) // 2],
-                    )
-                nc.sync.dma_start(out=h_block[j][:], in_=h_rows[:, :, j * N_TILE : (j + 1) * N_TILE])
+            load_scale("n", j, 0)
+            load_scale("n", j, 1)
+            load_h(j)
+            load_scale("n", j, 2)
+            load_scale("n", j, 3)
+            load_words("n", j)
+        j = COL_TILES - 1
+        load_scale("r", j, 0)
+        load_scale("r", j, 1)
+        load_gh("r", j)
+        load_scale("r", j, 2)
+        load_scale("r", j, 3)
+        load_words("r", j)
+        load_scale("z", j, 0)
+        load_scale("z", j, 1)
+        load_gh("z", j)
+        load_scale("z", j, 2)
+        load_scale("z", j, 3)
+        load_gh("n", j)
+        load_words("z", j)
+        load_scales("n", j)
+        load_last_words()
+        load_h(j)
 
         halves = 2
         for m in row_tiles:

@@ -144,14 +144,17 @@ def tile_grucellstack_pa_kernel(tc, x, h0, gh0, w_words, w_scales, b_ih0, out):
         load_words("r", j)
         load_scale("z", j, 0)
         load_scale("z", j, 1)
-        load_gh("z", j)
+        load_gh("n", j)
         load_scale("z", j, 2)
         load_scale("z", j, 3)
-        load_gh("n", j)
         load_words("z", j)
-        load_scales("n", j)
-        load_last_words()
+        load_scale("n", j, 0)
+        load_scale("n", j, 1)
+        load_gh("z", j)
+        load_scale("n", j, 2)
+        load_scale("n", j, 3)
         load_h(j)
+        load_last_words()
 
         halves = 2
         for m in row_tiles:
@@ -254,6 +257,9 @@ def tile_grucellstack_pa_kernel(tc, x, h0, gh0, w_words, w_scales, b_ih0, out):
             z_sum = [work.tile([P, N_TILE], F32, tag="z", name="z_sum") for m in row_tiles]
             for m in row_tiles:
                 nc.vector.tensor_tensor(out=z_sum[m][:], in0=bias_z[:], in1=gh_block[("z", j)][:, m, :], op=ALU.add)
+            if j == COL_TILES - 1:
+                bias_n = psum.tile([P, N_TILE], F32, tag="bank", name="bias_n")
+                nc.tensor.matmul(out=bias_n[:], lhsT=ones[:], rhs=bias_columns("n", j), start=True, stop=True)
             gi_z = gi_banks("z", j)
 
             z = [work.tile([P, N_TILE], F32, tag="zgate", name="zgate") for m in row_tiles]
@@ -266,8 +272,9 @@ def tile_grucellstack_pa_kernel(tc, x, h0, gh0, w_words, w_scales, b_ih0, out):
             for m in row_tiles:
                 nc.scalar.activation(out=z_rest[m][:], in_=z_sum[m][:], func=ACT.Sigmoid, scale=-1.0)
 
-            bias_n = psum.tile([P, N_TILE], F32, tag="bank", name="bias_n")
-            nc.tensor.matmul(out=bias_n[:], lhsT=ones[:], rhs=bias_columns("n", j), start=True, stop=True)
+            if j < COL_TILES - 1:
+                bias_n = psum.tile([P, N_TILE], F32, tag="bank", name="bias_n")
+                nc.tensor.matmul(out=bias_n[:], lhsT=ones[:], rhs=bias_columns("n", j), start=True, stop=True)
             gi_n = gi_banks("n", j) if j < COL_TILES - 1 else last_banks()
 
             n = [work.tile([P, N_TILE], F32, tag="n", name="n") for m in row_tiles]

from contextlib import ExitStack

import concourse.mybir as mybir
from concourse.masks import make_identity

F32 = mybir.dt.float32
BF16 = mybir.dt.bfloat16
I32 = mybir.dt.int32
U32 = mybir.dt.uint32
U8 = mybir.dt.uint8
FP8X4 = mybir.dt.float8_e4m3fn_x4
FP4X4 = mybir.dt.float4_e2m1fn_x4
ACT = mybir.ActivationFunctionType
ALU = mybir.AluOpType

P = 128
B, IN, L = 256, 2048, 1536
K_PASS = 4 * P
PASSES = IN // K_PASS
ROW_TILES = B // P
N_TILE = 512
COL_TILES = L // N_TILE
GATES = ("r", "z", "n")
GATE_COLUMN = {"r": 0, "z": L, "n": 2 * L}
QUADRANTS = 4
PSUM_BANKS = 8

FLOPS = 2 * B * IN * 3 * L


def tile_grucellstack_pa_kernel(tc, x, h0, gh0, w_words, w_scales, b_ih0, out):
    nc = tc.nc
    row_tiles = range(ROW_TILES)
    chunks = [(gate, j) for j in range(COL_TILES) for gate in GATES]

    with ExitStack() as stack:
        keep = stack.enter_context(tc.tile_pool(name="keep", bufs=1))
        work = stack.enter_context(tc.tile_pool(name="work", bufs=2 * ROW_TILES))
        psum = stack.enter_context(tc.psum_pool(name="psum", bufs=PSUM_BANKS))
        stack.enter_context(tc.manual_schedule())

        x_rows = [[keep.tile([P, IN // 2], BF16, name="x_rows%d_%d" % (m, half)) for half in range(2)] for m in row_tiles]
        x_grouped = [keep.tile([P, IN], BF16, name="x_grouped%d" % m, align_bytes=64) for m in row_tiles]
        x_codes = [keep.tile([P, IN // 4], U32, name="x_codes%d" % m, align_bytes=64) for m in row_tiles]
        x_scales = [keep.tile([P, IN // 4], U8, name="x_scales%d" % m, align_bytes=64) for m in row_tiles]
        w_codes = {}
        w_planes = {}
        gh_block = {}
        for gate, j in chunks:
            w_codes[(gate, j)] = keep.tile([P, PASSES, 2 * N_TILE], U8, name="w_codes_%s%d" % (gate, j), align_bytes=64)
            w_planes[(gate, j)] = keep.tile([P, PASSES, N_TILE], U8, name="w_plane_%s%d" % (gate, j), align_bytes=64)
            gh_block[(gate, j)] = keep.tile([P, ROW_TILES, N_TILE], BF16, name="gh_%s%d" % (gate, j))
        last_codes = [keep.tile([P, 2 * N_TILE], U8, name="last_codes%d" % g, align_bytes=64) for g in range(PASSES)]
        h_block = [keep.tile([P, ROW_TILES, N_TILE], BF16, name="h_%d" % j) for j in range(COL_TILES)]
        bias_row = keep.tile([P, 3 * L], BF16, name="bias_row")
        ones = keep.tile([P, P], BF16, name="ones")
        ident_bf16 = keep.tile([P, P], BF16, name="ident_bf16")
        ident_f32 = keep.tile([P, P], F32, name="ident_f32")
        table_in = keep.tile([P, 1], F32, name="table_in")
        table_out = keep.tile([P, 1], F32, name="table_out")

        nc.vector.memset(table_in[:], 0.0)
        nc.scalar.activation(out=table_out[:], in_=table_in[:], func=ACT.Sigmoid)
        nc.vector.memset(w_planes[chunks[0]][:].bitcast(I32), 0)
        nc.vector.memset(ones[:], 1.0)
        nc.vector.memset(bias_row[:].bitcast(I32), 0)
        for chunk in chunks[1 : len(GATES)]:
            nc.vector.memset(w_planes[chunk][:].bitcast(I32), 0)
        make_identity(nc, ident_f32[:])
        make_identity(nc, ident_bf16[:])
        for chunk in chunks[len(GATES) :]:
            nc.gpsimd.memset(w_planes[chunk][:].bitcast(F32), 0.0)

        scale_rows = w_scales.bitcast(I32).rearrange("g (Q s) c -> s Q g c", s=4)
        word_rows = w_words.bitcast(I32).rearrange("g p c -> p g c")
        gh_rows = gh0.rearrange("(m p) c -> p m c", p=P)
        h_rows = h0.rearrange("(m p) c -> p m c", p=P)

        def load_scales(gate, j):
            first = GATE_COLUMN[gate] + j * N_TILE
            plane_words = w_planes[(gate, j)][:].bitcast(I32)
            for s in range(4):
                nc.sync.dma_start(
                    out=plane_words[s : P : P // QUADRANTS, :, :],
                    in_=scale_rows[s][:, :, first // 4 : (first + N_TILE) // 4],
                )

        def load_words(gate, j):
            first = GATE_COLUMN[gate] + j * N_TILE
            nc.sync.dma_start(
                out=w_codes[(gate, j)][:].bitcast(I32),
                in_=word_rows[:, :, first // 2 : (first + N_TILE) // 2],
            )

        def load_gh(gate, j):
            first = GATE_COLUMN[gate] + j * N_TILE
            nc.sync.dma_start(out=gh_block[(gate, j)][:], in_=gh_rows[:, :, first : first + N_TILE])

        for m in row_tiles:
            for half in range(2):
                nc.sync.dma_start(out=x_rows[m][half][:], in_=x[m * P : (m + 1) * P, half * IN // 2 : (half + 1) * IN // 2])
        nc.sync.dma_start(out=bias_row[0:1, :], in_=b_ih0.rearrange("(o c) -> o c", o=1))
        def load_h(j):
            nc.sync.dma_start(out=h_block[j][:], in_=h_rows[:, :, j * N_TILE : (j + 1) * N_TILE])

        def load_last_words():
            first = GATE_COLUMN["n"] + (COL_TILES - 1) * N_TILE
            for g in range(PASSES):
                nc.sync.dma_start(out=last_codes[g][:].bitcast(I32), in_=word_rows[:, g, first // 2 : (first + N_TILE) // 2])

        def load_scale(gate, j, s):
            first = GATE_COLUMN[gate] + j * N_TILE
            nc.sync.dma_start(
                out=w_planes[(gate, j)][:].bitcast(I32)[s : P : P // QUADRANTS, :, :],
                in_=scale_rows[s][:, :, first // 4 : (first + N_TILE) // 4],
            )

        for j in range(COL_TILES - 1):
            load_scale("r", j, 0)
            load_scale("r", j, 1)
            load_gh("r", j)
            load_scale("r", j, 2)
            load_scale("r", j, 3)
            load_words("r", j)
            load_scale("z", j, 0)
            load_scale("z", j, 1)
            load_gh("z", j)
            load_scale("z", j, 2)
            load_scale("z", j, 3)
            load_gh("n", j)
            load_words("z", j)
            load_scale("n", j, 0)
            load_scale("n", j, 1)
            load_h(j)
            load_scale("n", j, 2)
            load_scale("n", j, 3)
            load_words("n", j)
        j = COL_TILES - 1
        load_scale("r", j, 0)
        load_scale("r", j, 1)
        load_gh("r", j)
        load_scale("r", j, 2)
        load_scale("r", j, 3)
        load_words("r", j)
        load_scale("z", j, 0)
        load_scale("z", j, 1)
        load_gh("n", j)
        load_scale("z", j, 2)
        load_scale("z", j, 3)
        load_words("z", j)
        load_scale("n", j, 0)
        load_scale("n", j, 1)
        load_gh("z", j)
        load_scale("n", j, 2)
        load_scale("n", j, 3)
        load_h(j)
        load_last_words()

        halves = 2
        for m in row_tiles:
            grouped_pairs = x_grouped[m][:].bitcast(F32)
            for half in range(halves):
                x_pairs = x_rows[m][half][:].bitcast(F32)
                flipped = psum.tile([P, N_TILE], F32, tag="bank", name="flipped")
                for slot in range(4):
                    g = slot // 2
                    u = slot % 2
                    nc.tensor.transpose(
                        out=flipped[:, slot * P : (slot + 1) * P],
                        in_=x_pairs[:, 256 * g + u : 256 * (g + 1) : 2],
                        identity=ident_f32[:],
                    )
                source = flipped[:].rearrange("p (g u b) -> p g b u", g=2, u=2)
                target = grouped_pairs[:, half * N_TILE : (half + 1) * N_TILE].rearrange(
                    "p (g b u) -> p g b u", g=2, u=2
                )
                if half == 0:
                    nc.vector.tensor_copy(out=target, in_=source)
                else:
                    nc.scalar.copy(out=target, in_=source)
        for m in row_tiles:
            for half in range(halves):
                values = slice(half * IN // 2, (half + 1) * IN // 2)
                words = slice(half * IN // 8, (half + 1) * IN // 8)
                nc.vector.quantize_mx(
                    out=x_codes[m][:, words].bitcast(FP8X4),
                    scales=x_scales[m][:, words],
                    in_=x_grouped[m][:, values],
                )

        def bias_columns(gate, j):
            first = GATE_COLUMN[gate] + j * N_TILE
            return bias_row[:, first : first + N_TILE]

        def gi_banks(gate, j):
            banks = []
            for m in row_tiles:
                acc = psum.tile([P, N_TILE], F32, tag="bank", name="acc")
                for g in range(PASSES):
                    rows = slice(g * P, (g + 1) * P)
                    nc.tensor.matmul_mx(
                        out=acc[:],
                        lhsT=x_codes[m][:, rows].bitcast(FP8X4),
                        lhsT_scale=x_scales[m][:, rows],
                        rhs=w_codes[(gate, j)][:, g, :].bitcast(FP4X4),
                        rhs_scale=w_planes[(gate, j)][:, g, :],
                        start=(g == 0),
                        stop=(g == PASSES - 1),
                    )
                banks.append(acc)
            return banks

        def last_banks():
            gate, j = "n", COL_TILES - 1
            banks = [psum.tile([P, N_TILE], F32, tag="bank", name="acc") for m in row_tiles]
            for g in range(PASSES):
                rows = slice(g * P, (g + 1) * P)
                for m in row_tiles:
                    nc.tensor.matmul_mx(
                        out=banks[m][:],
                        lhsT=x_codes[m][:, rows].bitcast(FP8X4),
                        lhsT_scale=x_scales[m][:, rows],
                        rhs=last_codes[g][:].bitcast(FP4X4),
                        rhs_scale=w_planes[(gate, j)][:, g, :],
                        start=(g == 0),
                        stop=(g == PASSES - 1),
                    )
            return banks

        def gh_plus_bias(gate, j):
            totals = []
            for m in row_tiles:
                bank = psum.tile([P, N_TILE], F32, tag="bank", name="gh_bias")
                nc.tensor.matmul(out=bank[:], lhsT=ident_bf16[:], rhs=gh_block[(gate, j)][:, m, :], start=True, stop=False)
                nc.tensor.matmul(out=bank[:], lhsT=ones[:], rhs=bias_columns(gate, j), start=False, stop=True)
                total = work.tile([P, N_TILE], F32, tag=gate, name="gate_" + gate)
                nc.scalar.copy(out=total[:], in_=bank[:])
                totals.append(total)
            return totals

        def sigmoid_of_sum(banks, totals):
            for m in row_tiles:
                nc.vector.tensor_tensor(out=totals[m][:], in0=banks[m][:], in1=totals[m][:], op=ALU.add)
                nc.scalar.activation(out=totals[m][:], in_=totals[m][:], func=ACT.Sigmoid)

        for j in range(COL_TILES):
            r = gh_plus_bias("r", j)
            gi_r = gi_banks("r", j)
            side = [work.tile([P, N_TILE], F32, tag="side", name="side") for m in row_tiles]
            for m in row_tiles:
                nc.vector.tensor_tensor(out=r[m][:], in0=gi_r[m][:], in1=r[m][:], op=ALU.add)
                nc.scalar.activation(out=r[m][:], in_=r[m][:], func=ACT.Sigmoid)
                nc.gpsimd.tensor_tensor(out=side[m][:], in0=r[m][:], in1=gh_block[("n", j)][:, m, :], op=ALU.mult)

            bias_z = psum.tile([P, N_TILE], F32, tag="bank", name="bias_z")
            nc.tensor.matmul(out=bias_z[:], lhsT=ones[:], rhs=bias_columns("z", j), start=True, stop=True)
            z_sum = [work.tile([P, N_TILE], F32, tag="z", name="z_sum") for m in row_tiles]
            for m in row_tiles:
                nc.vector.tensor_tensor(out=z_sum[m][:], in0=bias_z[:], in1=gh_block[("z", j)][:, m, :], op=ALU.add)
            if j == COL_TILES - 1:
                bias_n = psum.tile([P, N_TILE], F32, tag="bank", name="bias_n")
                nc.tensor.matmul(out=bias_n[:], lhsT=ones[:], rhs=bias_columns("n", j), start=True, stop=True)
            gi_z = gi_banks("z", j)

            z = [work.tile([P, N_TILE], F32, tag="zgate", name="zgate") for m in row_tiles]
            z_rest = [work.tile([P, N_TILE], F32, tag="zrest", name="zrest") for m in row_tiles]
            z_h = [work.tile([P, N_TILE], F32, tag="zh", name="zh") for m in row_tiles]
            for m in row_tiles:
                nc.vector.tensor_tensor(out=z_sum[m][:], in0=gi_z[m][:], in1=z_sum[m][:], op=ALU.add)
                nc.scalar.activation(out=z[m][:], in_=z_sum[m][:], func=ACT.Sigmoid)
                nc.gpsimd.tensor_tensor(out=z_h[m][:], in0=z[m][:], in1=h_block[j][:, m, :], op=ALU.mult)
            for m in row_tiles:
                nc.scalar.activation(out=z_rest[m][:], in_=z_sum[m][:], func=ACT.Sigmoid, scale=-1.0)

            if j < COL_TILES - 1:
                bias_n = psum.tile([P, N_TILE], F32, tag="bank", name="bias_n")
                nc.tensor.matmul(out=bias_n[:], lhsT=ones[:], rhs=bias_columns("n", j), start=True, stop=True)
            gi_n = gi_banks("n", j) if j < COL_TILES - 1 else last_banks()

            n = [work.tile([P, N_TILE], F32, tag="n", name="n") for m in row_tiles]
            for m in row_tiles:
                nc.vector.tensor_tensor(out=side[m][:], in0=bias_n[:], in1=side[m][:], op=ALU.add)
            for m in row_tiles:
                nc.vector.tensor_tensor(out=n[m][:], in0=gi_n[m][:], in1=side[m][:], op=ALU.add)
                nc.scalar.activation(out=n[m][:], in_=n[m][:], func=ACT.Tanh)

            for m in row_tiles:
                nc.vector.tensor_tensor(out=n[m][:], in0=z_rest[m][:], in1=n[m][:], op=ALU.mult)
            for m in row_tiles:
                nc.vector.tensor_tensor(out=n[m][:], in0=n[m][:], in1=z_h[m][:], op=ALU.add)
                nc.sync.dma_start(out=out[m * P : (m + 1) * P, j * N_TILE : (j + 1) * N_TILE], in_=n[m][:])
